import numpy as np
import ml_dtypes


def mxq(x, axis, fmt="e4m3"):
    dtype, down = {"e4m3": (ml_dtypes.float8_e4m3fn, 7), "e5m2": (ml_dtypes.float8_e5m2, 14)}[fmt]
    v = np.moveaxis(np.asarray(x, np.float32).astype(ml_dtypes.bfloat16).astype(np.float64), axis, -1)
    blocks = v.reshape(v.shape[:-1] + (-1, 32))
    amax = np.abs(blocks).max(-1, keepdims=True)
    byte = np.maximum(np.where(amax > 0, np.frexp(amax)[1] - 1 + 127, 0) - down, 1)
    scale = np.exp2(byte - 127.0)
    codes = (blocks / scale).astype(np.float32).astype(dtype).astype(np.float64)
    return np.moveaxis((codes * scale).reshape(v.shape), -1, axis)


WIDE = False


def mx_kscale(k):
    if not WIDE:
        return np.ones(k)
    levels = np.array([10, -10, 5, -5, 0])
    a = np.random.permutation(np.resize(levels, k // 512 * 4)).reshape(k // 512, 4)
    idx = np.arange(k)
    return np.exp2(a[idx // 512, idx % 128 // 32])


BF16 = ml_dtypes.bfloat16


def bf(x):
    return np.asarray(x, np.float32).astype(BF16)


def f64(x):
    return np.asarray(x).astype(np.float64)


N, MI0, MI1, MS, MG, MO0, MO1, DV = 4096, 128, 128, 512, 512, 256, 256, 3
EPS = 1e-5


def irlin_mx(x, mul0, mul1, w0, w1):
    n = x.shape[0]
    x0 = x[:, :mul0]
    x1 = x[:, mul0:].reshape(n, mul1, DV).transpose(0, 2, 1)
    y0 = (mxq(x0, 1, "e4m3") @ mxq(w0, 0, "e4m3")) * (1.0 / np.sqrt(mul0))
    y1 = (mxq(x1, 2, "e4m3") @ mxq(w1, 0, "e4m3")).transpose(0, 2, 1) * (1.0 / np.sqrt(mul1))
    return np.concatenate([y0, y1.reshape(n, -1)], axis=-1)


def irlin_plain(x, mul0, mul1, w0, w1):
    n = x.shape[0]
    x0 = x[:, :mul0]
    x1 = x[:, mul0:].reshape(n, mul1, DV).transpose(0, 2, 1)
    y0 = (x0 @ w0) * (1.0 / np.sqrt(mul0))
    y1 = (x1 @ w1).transpose(0, 2, 1) * (1.0 / np.sqrt(mul1))
    return np.concatenate([y0, y1.reshape(n, -1)], axis=-1)


def batchnorm(x, w, b):
    n = x.shape[0]
    s = x[:, :MO0]
    v = x[:, MO0:].reshape(n, MO1, DV)
    s = s - s.mean(0)
    s_inv = 1.0 / np.sqrt((s * s).mean(0) + EPS)
    s = s * (s_inv * w[:MO0]) + b
    v_inv = 1.0 / np.sqrt((v * v).mean(-1).mean(0) + EPS)
    v = v * (v_inv * w[MO0:])[None, :, None]
    return np.concatenate([s, v.reshape(n, -1)], axis=-1)


def setup_inputs():
    s0, s1 = mx_kscale(MS), mx_kscale(MG)
    h0 = (0.1 + 0.3 * np.random.standard_normal((N, MS))) * s0
    h1 = 0.28 * np.random.standard_normal((N, MG, DV)) * s1[None, :, None]
    return {"h2": bf(np.concatenate([h0, h1.reshape(N, -1)], axis=-1)),
            "features": bf(np.random.standard_normal((N, MI0 + DV * MI1))),
            "lin3_W0": bf(np.random.standard_normal((MS, MO0)) / s0[:, None]),
            "lin3_W1": bf(np.random.standard_normal((MG, MO1)) / s1[:, None]),
            "byp_W0": bf(np.random.standard_normal((MI0, MO0))),
            "byp_W1": bf(np.random.standard_normal((MI1, MO1))),
            "bn_weight": bf(1.0 + 0.1 * np.random.standard_normal(MO0 + MO1)),
            "bn_bias": bf(0.1 * np.random.standard_normal(MO0))}


def reference(h2, features, lin3_W0, lin3_W1, byp_W0, byp_W1, bn_weight, bn_bias):
    out = irlin_mx(f64(h2), MS, MG, f64(lin3_W0), f64(lin3_W1))
    out = out + irlin_plain(f64(features), MI0, MI1, f64(byp_W0), f64(byp_W1))
    return batchnorm(out, f64(bn_weight), f64(bn_bias))

@@ -1,0 +1,306 @@
+from contextlib import ExitStack
+import math
+
+import concourse.mybir as mybir
+from concourse.masks import make_identity
+
+F32 = mybir.dt.float32
+BF16 = mybir.dt.bfloat16
+U32 = mybir.dt.uint32
+U8 = mybir.dt.uint8
+FP8X4 = mybir.dt.float8_e4m3fn_x4
+ALU = mybir.AluOpType
+
+P = 128
+NODES = 4096
+DV = 3
+SECTIONS = 1 + DV
+HID = 512
+INP = 128
+OUTC = 256
+HALVES = OUTC // P
+GROUP = 512
+J = GROUP // P
+GROUPS = NODES // GROUP
+STATS = 6
+EPS = 1e-5
+
+FLOPS = 2 * NODES * SECTIONS * OUTC * (HID + INP)
+
+
+def quantise_weight(nc, pool, w, label):
+    raw = pool.tile([P, 4, OUTC], BF16, name="w_raw")
+    for u in range(2):
+        nc.scalar.dma_start(
+            out=raw[:, 2 * u : 2 * u + 2, :],
+            in_=w[256 * u : 256 * (u + 1), :].rearrange("(p e) c -> p e c", e=2),
+        )
+    grouped = pool.tile([P, OUTC, 4], BF16, name="w_grouped", align_bytes=64)
+    nc.vector.tensor_copy(out=grouped[:], in_=raw[:].rearrange("p t c -> p c t"))
+    codes = pool.tile([P, OUTC], U32, name=label + "_codes", align_bytes=64)
+    scales = pool.tile([P, OUTC], U8, name=label + "_scales", align_bytes=64)
+    nc.vector.quantize_mx(
+        out=codes[:].bitcast(FP8X4),
+        scales=scales[:],
+        in_=grouped[:].rearrange("p c t -> p (c t)"),
+    )
+    return codes, scales
+
+
+def tile_feedforward_pb_t_kernel(
+    tc, h2, features, lin3_W0, lin3_W1, byp_W0, byp_W1, bn_weight, bn_bias, out
+):
+    nc = tc.nc
+    with ExitStack() as whole:
+        consts = whole.enter_context(tc.tile_pool(name="consts", bufs=1))
+        y_pool = whole.enter_context(tc.tile_pool(name="y", bufs=1))
+
+        ident_f32 = consts.tile([P, P], F32)
+        make_identity(nc, ident_f32[:])
+        ident_bf16 = consts.tile([P, P], BF16)
+        make_identity(nc, ident_bf16[:])
+
+        warm = consts.tile([P, 1], F32)
+        nc.vector.memset(warm[:], 1.0)
+        nc.scalar.sqrt(out=warm[:], in_=warm[:])
+
+        lin_w = [
+            quantise_weight(nc, consts, lin3_W0, "w0"),
+            quantise_weight(nc, consts, lin3_W1, "w1"),
+        ]
+        byp_w = []
+        for label, w in (("byp0", byp_W0), ("byp1", byp_W1)):
+            w_sb = consts.tile([P, OUTC], BF16, name=label)
+            nc.scalar.dma_start(out=w_sb[:], in_=w)
+            byp_w.append(w_sb)
+
+        bn_rows = consts.tile([P, P], BF16)
+        nc.vector.memset(bn_rows[:], 0.0)
+        nc.scalar.dma_start(out=bn_rows[0:4, :], in_=bn_weight.rearrange("(r c) -> r c", c=P))
+        nc.scalar.dma_start(out=bn_rows[4:6, :], in_=bn_bias.rearrange("(r c) -> r c", c=P))
+        bn_cols = consts.tile([P, 6], F32)
+
+        y = [y_pool.tile([P, HALVES, SECTIONS, GROUP], F32, name="y%d" % g) for g in range(GROUPS)]
+        stats_scal = consts.tile([P, HALVES, GROUPS, STATS], F32)
+        stats_vec = consts.tile([P, HALVES, GROUPS * DV, STATS], F32)
+
+        with ExitStack() as phase1:
+            stage = phase1.enter_context(tc.tile_pool(name="stage", bufs=2))
+            work = phase1.enter_context(tc.tile_pool(name="work", bufs=3))
+            psum_x = phase1.enter_context(tc.psum_pool(name="psum_x", bufs=2))
+            psum_f = phase1.enter_context(tc.psum_pool(name="psum_f", bufs=2))
+            psum_mx = phase1.enter_context(tc.psum_pool(name="psum_mx", bufs=2))
+            psum_byp = phase1.enter_context(tc.psum_pool(name="psum_byp", bufs=2))
+
+            bn_ps = psum_f.tile([P, P], BF16, tag="feat_ps")
+            nc.tensor.transpose(bn_ps[:], bn_rows[:], ident_bf16[:])
+            nc.vector.tensor_copy(out=bn_cols[:], in_=bn_ps[:, 0:6])
+
+            loaded = {}
+
+            def load(g):
+                rows = slice(g * GROUP, (g + 1) * GROUP)
+                h2_scal = stage.tile([P, J, HID], BF16, name="h2_scal")
+                nc.sync.dma_start(
+                    out=h2_scal[:], in_=h2[rows, 0:HID].rearrange("(p j) k -> p j k", j=J)
+                )
+                feat = stage.tile([P, J, SECTIONS * INP], BF16, name="feat")
+                nc.sync.dma_start(
+                    out=feat[:], in_=features[rows, :].rearrange("(p j) k -> p j k", j=J)
+                )
+                h2_vec = stage.tile([P, J, DV * HID], BF16, name="h2_vec")
+                nc.sync.dma_start(
+                    out=h2_vec[:], in_=h2[rows, HID:].rearrange("(p j) k -> p j k", j=J)
+                )
+                loaded[g] = (h2_scal, feat, h2_vec)
+
+            def prepare(g, s):
+                h2_scal, feat, h2_vec = loaded[g]
+                if s == 0:
+                    hidden = h2_scal
+                else:
+                    hidden = stage.tile([P, J, HID], BF16, name="h2_comp", bufs=5)
+                    nc.gpsimd.tensor_scalar(
+                        out=hidden[:],
+                        in0=h2_vec[:].rearrange("p j (i d) -> p d j i", d=DV)[:, s - 1],
+                        scalar1=1.0,
+                        scalar2=0.0,
+                        op0=ALU.mult,
+                        op1=ALU.add,
+                    )
+                grouped = work.tile([P, GROUP, 2], F32, name="grouped", align_bytes=64)
+                for half in range(2):
+                    hid_ps = psum_x.tile([P, 2, 2 * P], F32, name="hid_ps")
+                    for jj in range(2):
+                        words = hidden[:, 2 * half + jj, :].bitcast(F32)
+                        for u in range(2):
+                            nc.tensor.transpose(
+                                hid_ps[:, u, jj * P : (jj + 1) * P],
+                                words[:, u * P : (u + 1) * P],
+                                ident_f32[:],
+                            )
+                    nc.scalar.copy(
+                        out=grouped[:, half * 2 * P : (half + 1) * 2 * P, :],
+                        in_=hid_ps[:].rearrange("p u n -> p n u"),
+                    )
+                codes = work.tile([P, GROUP], U32, name="codes", align_bytes=64)
+                scales = work.tile([P, GROUP], U8, name="scales", align_bytes=64)
+                nc.vector.quantize_mx(
+                    out=codes[:].bitcast(FP8X4),
+                    scales=scales[:],
+                    in_=grouped[:].rearrange("p n w -> p (n w)").bitcast(BF16),
+                )
+                feat_ps = psum_f.tile([P, GROUP], BF16, name="feat_ps")
+                for j in range(J):
+                    if s == 0:
+                        cols = feat[:, j, 0:INP]
+                    else:
+                        cols = feat[:, j, INP:].rearrange("p (i d) -> p d i", d=DV)[:, s - 1]
+                    nc.tensor.transpose(feat_ps[:, j * P : (j + 1) * P], cols, ident_bf16[:])
+                featT = work.tile([P, GROUP], BF16, name="featT")
+                nc.scalar.copy(out=featT[:], in_=feat_ps[:])
+                return codes, scales, featT
+
+            def multiply(g, s, operands):
+                codes, scales, featT = operands
+                kind = min(s, 1)
+                w_codes, w_scales = lin_w[kind]
+                sums = []
+                for h in range(HALVES):
+                    chans = slice(h * P, (h + 1) * P)
+                    mx_ps = psum_mx.tile([P, GROUP], F32, name="mx_ps")
+                    nc.tensor.matmul_mx(
+                        out=mx_ps[:],
+                        lhsT=w_codes[:, chans].bitcast(FP8X4),
+                        lhsT_scale=w_scales[:, chans],
+                        rhs=codes[:].bitcast(FP8X4),
+                        rhs_scale=scales[:],
+                        start=True,
+                        stop=True,
+                    )
+                    sums.append(mx_ps)
+                for h in range(HALVES):
+                    chans = slice(h * P, (h + 1) * P)
+                    byp_ps = psum_byp.tile([P, GROUP], F32, name="byp_ps")
+                    nc.tensor.matmul(
+                        out=byp_ps[:], lhsT=byp_w[kind][:, chans], rhs=featT[:], start=True, stop=True
+                    )
+                    byp_sb = work.tile([P, GROUP], F32, name="byp_sb")
+                    nc.scalar.mul(out=byp_sb[:], in_=byp_ps[:], mul=1.0 / math.sqrt(INP))
+                    nc.vector.scalar_tensor_tensor(
+                        out=y[g][:, h, s, :],
+                        in0=sums[h][:],
+                        scalar=1.0 / math.sqrt(HID),
+                        in1=byp_sb[:],
+                        op0=ALU.mult,
+                        op1=ALU.add,
+                    )
+                for h in range(HALVES):
+                    if s == 0:
+                        chunk = stats_scal[:, h, g, :]
+                    else:
+                        chunk = stats_vec[:, h, g * DV + s - 1, :]
+                    nc.vector.bn_stats(out=chunk, in_=y[g][:, h, s, :])
+
+            todo = [(g, s) for g in range(GROUPS) for s in range(SECTIONS)]
+            load(0)
+            load(1)
+            ready = prepare(*todo[0])
+            for i in range(1, len(todo)):
+                g, s = todo[i]
+                if s == 0 and g + 1 < GROUPS:
+                    load(g + 1)
+                following = prepare(g, s)
+                multiply(todo[i - 1][0], todo[i - 1][1], ready)
+                ready = following
+            multiply(todo[-1][0], todo[-1][1], ready)
+
+        moments = consts.tile([P, 2 * HALVES, 2], F32)
+        for h in range(HALVES):
+            nc.vector.bn_aggr(
+                out=moments[:, h, :], in_=stats_scal[:, h].rearrange("p c s -> p (c s)")
+            )
+            nc.vector.bn_aggr(
+                out=moments[:, HALVES + h, :], in_=stats_vec[:, h].rearrange("p c s -> p (c s)")
+            )
+        mean_sq = consts.tile([P, HALVES], F32)
+        nc.vector.tensor_mul(out=mean_sq[:], in0=moments[:, HALVES:, 0], in1=moments[:, HALVES:, 0])
+        spread = consts.tile([P, 2 * HALVES], F32)
+        nc.vector.tensor_scalar_add(out=spread[:, 0:HALVES], in0=moments[:, 0:HALVES, 1], scalar1=EPS)
+        nc.vector.scalar_tensor_tensor(
+            out=spread[:, HALVES:],
+            in0=moments[:, HALVES:, 1],
+            scalar=EPS,
+            in1=mean_sq[:],
+            op0=ALU.add,
+            op1=ALU.add,
+        )
+        root = consts.tile([P, 2 * HALVES], F32)
+        nc.scalar.sqrt(out=root[:], in_=spread[:])
+        scale = consts.tile([P, 2 * HALVES], F32)
+        nc.vector.reciprocal(out=scale[:], in_=root[:])
+        nc.vector.tensor_mul(out=scale[:], in0=scale[:], in1=bn_cols[:, 0 : 2 * HALVES])
+        shift = consts.tile([P, 2 * HALVES], F32)
+        nc.vector.memset(shift[:], 0.0)
+        scaled_mean = consts.tile([P, HALVES], F32)
+        nc.vector.tensor_mul(out=scaled_mean[:], in0=moments[:, 0:HALVES, 0], in1=scale[:, 0:HALVES])
+        nc.vector.tensor_sub(
+            out=shift[:, 0:HALVES], in0=bn_cols[:, 2 * HALVES : 3 * HALVES], in1=scaled_mean[:]
+        )
+
+        with ExitStack() as phase2:
+            rows_pool = phase2.enter_context(tc.tile_pool(name="rows", bufs=3))
+            psum_s = phase2.enter_context(tc.psum_pool(name="psum_s", bufs=2))
+            psum_v = phase2.enter_context(tc.psum_pool(name="psum_v", bufs=6))
+
+            def normalise(g):
+                for h in range(HALVES):
+                    nc.vector.tensor_scalar(
+                        out=y[g][:, h, 0, :],
+                        in0=y[g][:, h, 0, :],
+                        scalar1=scale[:, h : h + 1],
+                        scalar2=shift[:, h : h + 1],
+                        op0=ALU.mult,
+                        op1=ALU.add,
+                    )
+                    b = HALVES + h
+                    nc.gpsimd.tensor_scalar(
+                        out=y[g][:, h, 1:, :],
+                        in0=y[g][:, h, 1:, :],
+                        scalar1=scale[:, b : b + 1],
+                        scalar2=shift[:, b : b + 1],
+                        op0=ALU.mult,
+                        op1=ALU.add,
+                    )
+
+            def store(g, half):
+                rows_sb = rows_pool.tile([P, 2, SECTIONS * OUTC], F32, name="rows_sb")
+                scal_ps = psum_s.tile([P, 2, HALVES, P], F32, name="scal_ps")
+                for jj in range(2):
+                    nodes = slice((2 * half + jj) * P, (2 * half + jj + 1) * P)
+                    for h in range(HALVES):
+                        nc.tensor.transpose(scal_ps[:, jj, h, :], y[g][:, h, 0, nodes], ident_f32[:])
+                nc.vector.tensor_copy(
+                    out=rows_sb[:, :, 0:OUTC], in_=scal_ps[:].rearrange("p j h c -> p j (h c)")
+                )
+                for jj in range(2):
+                    nodes = slice((2 * half + jj) * P, (2 * half + jj + 1) * P)
+                    for h in range(HALVES):
+                        vec_ps = psum_v.tile([P, DV, P], F32, name="vec_ps")
+                        for d in range(DV):
+                            nc.tensor.transpose(vec_ps[:, d, :], y[g][:, h, 1 + d, nodes], ident_f32[:])
+                        first = OUTC + h * DV * P
+                        dest = rows_sb[:, jj, first : first + DV * P].rearrange("p (o d) -> p o d", d=DV)
+                        if jj == 0 and h == 0:
+                            nc.vector.tensor_copy(out=dest, in_=vec_ps[:].rearrange("p d o -> p o d"))
+                        else:
+                            nc.scalar.copy(out=dest, in_=vec_ps[:].rearrange("p d o -> p o d"))
+                group_rows = out[g * GROUP : (g + 1) * GROUP, :].rearrange("(p j) c -> p j c", j=J)
+                nc.sync.dma_start(out=group_rows[:, 2 * half : 2 * half + 2, :], in_=rows_sb[:])
+
+            normalise(0)
+            for g in range(GROUPS):
+                if g + 1 < GROUPS:
+                    normalise(g + 1)
+                for half in range(2):
+                    store(g, half)

@@ -10,6 +10,7 @@ U32 = mybir.dt.uint32
 U8 = mybir.dt.uint8
 FP8X4 = mybir.dt.float8_e4m3fn_x4
 ALU = mybir.AluOpType
+ACT = mybir.ActivationFunctionType
 
 P = 128
 NODES = 4096
@@ -120,16 +121,18 @@ def tile_feedforward_pb_t_kernel(
                     hidden = h2_scal
                 else:
                     hidden = stage.tile([P, J, HID], BF16, name="h2_comp", bufs=5)
-                    nc.gpsimd.tensor_scalar(
-                        out=hidden[:],
-                        in0=h2_vec[:].rearrange("p j (i d) -> p d j i", d=DV)[:, s - 1],
-                        scalar1=1.0,
-                        scalar2=0.0,
-                        op0=ALU.mult,
-                        op1=ALU.add,
-                    )
                 grouped = work.tile([P, GROUP, 2], F32, name="grouped", align_bytes=64)
                 for half in range(2):
+                    if s > 0:
+                        pair = slice(2 * half, 2 * half + 2)
+                        nc.gpsimd.tensor_scalar(
+                            out=hidden[:, pair, :],
+                            in0=h2_vec[:, pair, :].rearrange("p j (i d) -> p d j i", d=DV)[:, s - 1],
+                            scalar1=1.0,
+                            scalar2=0.0,
+                            op0=ALU.mult,
+                            op1=ALU.add,
+                        )
                     hid_ps = psum_x.tile([P, 2, 2 * P], F32, name="hid_ps")
                     for jj in range(2):
                         words = hidden[:, 2 * half + jj, :].bitcast(F32)
@@ -165,7 +168,16 @@ def tile_feedforward_pb_t_kernel(
                 codes, scales, featT = operands
                 kind = min(s, 1)
                 w_codes, w_scales = lin_w[kind]
-                sums = []
+                bypass = []
+                for h in range(HALVES):
+                    chans = slice(h * P, (h + 1) * P)
+                    byp_ps = psum_byp.tile([P, GROUP], F32, name="byp_ps")
+                    nc.tensor.matmul(
+                        out=byp_ps[:], lhsT=byp_w[kind][:, chans], rhs=featT[:], start=True, stop=True
+                    )
+                    byp_sb = work.tile([P, GROUP], F32, name="byp_sb")
+                    nc.scalar.mul(out=byp_sb[:], in_=byp_ps[:], mul=1.0 / math.sqrt(INP))
+                    bypass.append(byp_sb)
                 for h in range(HALVES):
                     chans = slice(h * P, (h + 1) * P)
                     mx_ps = psum_mx.tile([P, GROUP], F32, name="mx_ps")
@@ -178,20 +190,11 @@ def tile_feedforward_pb_t_kernel(
                         start=True,
                         stop=True,
                     )
-                    sums.append(mx_ps)
-                for h in range(HALVES):
-                    chans = slice(h * P, (h + 1) * P)
-                    byp_ps = psum_byp.tile([P, GROUP], F32, name="byp_ps")
-                    nc.tensor.matmul(
-                        out=byp_ps[:], lhsT=byp_w[kind][:, chans], rhs=featT[:], start=True, stop=True
-                    )
-                    byp_sb = work.tile([P, GROUP], F32, name="byp_sb")
-                    nc.scalar.mul(out=byp_sb[:], in_=byp_ps[:], mul=1.0 / math.sqrt(INP))
                     nc.vector.scalar_tensor_tensor(
                         out=y[g][:, h, s, :],
-                        in0=sums[h][:],
+                        in0=mx_ps[:],
                         scalar=1.0 / math.sqrt(HID),
-                        in1=byp_sb[:],
+                        in1=bypass[h][:],
                         op0=ALU.mult,
                         op1=ALU.add,
                     )
@@ -255,13 +258,12 @@ def tile_feedforward_pb_t_kernel(
 
             def normalise(g):
                 for h in range(HALVES):
-                    nc.vector.tensor_scalar(
+                    nc.scalar.activation(
                         out=y[g][:, h, 0, :],
-                        in0=y[g][:, h, 0, :],
-                        scalar1=scale[:, h : h + 1],
-                        scalar2=shift[:, h : h + 1],
-                        op0=ALU.mult,
-                        op1=ALU.add,
+                        in_=y[g][:, h, 0, :],
+                        func=ACT.Identity,
+                        scale=scale[:, h : h + 1],
+                        bias=shift[:, h : h + 1],
                     )
                     b = HALVES + h
                     nc.gpsimd.tensor_scalar(
@@ -291,7 +293,7 @@ def tile_feedforward_pb_t_kernel(
                             nc.tensor.transpose(vec_ps[:, d, :], y[g][:, h, 1 + d, nodes], ident_f32[:])
                         first = OUTC + h * DV * P
                         dest = rows_sb[:, jj, first : first + DV * P].rearrange("p (o d) -> p o d", d=DV)
-                        if jj == 0 and h == 0:
+                        if h == 0:
                             nc.vector.tensor_copy(out=dest, in_=vec_ps[:].rearrange("p d o -> p o d"))
                         else:
                             nc.scalar.copy(out=dest, in_=vec_ps[:].rearrange("p d o -> p o d"))

@@ -115,89 +115,100 @@ def tile_feedforward_pb_t_kernel(
                 )
                 loaded[g] = (h2_scal, feat, h2_vec)
 
-            def prepare(g, s):
+            def open_section(g, s):
                 h2_scal, feat, h2_vec = loaded[g]
                 if s == 0:
                     hidden = h2_scal
                 else:
                     hidden = stage.tile([P, J, HID], BF16, name="h2_comp", bufs=5)
-                grouped = work.tile([P, GROUP, 2], F32, name="grouped", align_bytes=64)
-                for half in range(2):
-                    if s > 0:
-                        pair = slice(2 * half, 2 * half + 2)
-                        nc.gpsimd.tensor_scalar(
-                            out=hidden[:, pair, :],
-                            in0=h2_vec[:, pair, :].rearrange("p j (i d) -> p d j i", d=DV)[:, s - 1],
-                            scalar1=1.0,
-                            scalar2=0.0,
-                            op0=ALU.mult,
-                            op1=ALU.add,
-                        )
-                    hid_ps = psum_x.tile([P, 2, 2 * P], F32, name="hid_ps")
-                    for jj in range(2):
-                        words = hidden[:, 2 * half + jj, :].bitcast(F32)
-                        for u in range(2):
-                            nc.tensor.transpose(
-                                hid_ps[:, u, jj * P : (jj + 1) * P],
-                                words[:, u * P : (u + 1) * P],
-                                ident_f32[:],
-                            )
-                    nc.scalar.copy(
-                        out=grouped[:, half * 2 * P : (half + 1) * 2 * P, :],
-                        in_=hid_ps[:].rearrange("p u n -> p n u"),
+                return {
+                    "g": g,
+                    "s": s,
+                    "hidden": hidden,
+                    "grouped": work.tile([P, GROUP, 2], F32, name="grouped", align_bytes=64),
+                    "feat_ps": psum_f.tile([P, GROUP], BF16, name="feat_ps"),
+                }
+
+            def transpose_half(sec, half):
+                h2_scal, feat, h2_vec = loaded[sec["g"]]
+                s = sec["s"]
+                hidden = sec["hidden"]
+                pair = slice(2 * half, 2 * half + 2)
+                if s > 0:
+                    nc.gpsimd.tensor_scalar(
+                        out=hidden[:, pair, :],
+                        in0=h2_vec[:, pair, :].rearrange("p j (i d) -> p d j i", d=DV)[:, s - 1],
+                        scalar1=1.0,
+                        scalar2=0.0,
+                        op0=ALU.mult,
+                        op1=ALU.add,
                     )
+                hid_ps = psum_x.tile([P, 2, 2 * P], F32, name="hid_ps")
+                for jj in range(2):
+                    words = hidden[:, 2 * half + jj, :].bitcast(F32)
+                    for u in range(2):
+                        nc.tensor.transpose(
+                            hid_ps[:, u, jj * P : (jj + 1) * P],
+                            words[:, u * P : (u + 1) * P],
+                            ident_f32[:],
+                        )
+                nc.scalar.copy(
+                    out=sec["grouped"][:, half * 2 * P : (half + 1) * 2 * P, :],
+                    in_=hid_ps[:].rearrange("p u n -> p n u"),
+                )
+                for j in range(2 * half, 2 * half + 2):
+                    if s == 0:
+                        cols = feat[:, j, 0:INP]
+                    else:
+                        cols = feat[:, j, INP:].rearrange("p (i d) -> p d i", d=DV)[:, s - 1]
+                    nc.tensor.transpose(sec["feat_ps"][:, j * P : (j + 1) * P], cols, ident_bf16[:])
+
+            def close_section(sec):
+                featT = work.tile([P, GROUP], BF16, name="featT")
+                nc.scalar.copy(out=featT[:], in_=sec["feat_ps"][:])
                 codes = work.tile([P, GROUP], U32, name="codes", align_bytes=64)
                 scales = work.tile([P, GROUP], U8, name="scales", align_bytes=64)
                 nc.vector.quantize_mx(
                     out=codes[:].bitcast(FP8X4),
                     scales=scales[:],
-                    in_=grouped[:].rearrange("p n w -> p (n w)").bitcast(BF16),
+                    in_=sec["grouped"][:].rearrange("p n w -> p (n w)").bitcast(BF16),
                 )
-                feat_ps = psum_f.tile([P, GROUP], BF16, name="feat_ps")
-                for j in range(J):
-                    if s == 0:
-                        cols = feat[:, j, 0:INP]
-                    else:
-                        cols = feat[:, j, INP:].rearrange("p (i d) -> p d i", d=DV)[:, s - 1]
-                    nc.tensor.transpose(feat_ps[:, j * P : (j + 1) * P], cols, ident_bf16[:])
-                featT = work.tile([P, GROUP], BF16, name="featT")
-                nc.scalar.copy(out=featT[:], in_=feat_ps[:])
-                return codes, scales, featT
+                sec["featT"] = featT
+                sec["codes"] = codes
+                sec["scales"] = scales
 
-            def multiply(g, s, operands):
-                codes, scales, featT = operands
+            def multiply_half(sec, h):
+                g, s = sec["g"], sec["s"]
                 kind = min(s, 1)
                 w_codes, w_scales = lin_w[kind]
-                bypass = []
-                for h in range(HALVES):
-                    chans = slice(h * P, (h + 1) * P)
-                    byp_ps = psum_byp.tile([P, GROUP], F32, name="byp_ps")
-                    nc.tensor.matmul(
-                        out=byp_ps[:], lhsT=byp_w[kind][:, chans], rhs=featT[:], start=True, stop=True
-                    )
-                    byp_sb = work.tile([P, GROUP], F32, name="byp_sb")
-                    nc.scalar.mul(out=byp_sb[:], in_=byp_ps[:], mul=1.0 / math.sqrt(INP))
-                    bypass.append(byp_sb)
-                for h in range(HALVES):
-                    chans = slice(h * P, (h + 1) * P)
-                    mx_ps = psum_mx.tile([P, GROUP], F32, name="mx_ps")
-                    nc.tensor.matmul_mx(
-                        out=mx_ps[:],
-                        lhsT=w_codes[:, chans].bitcast(FP8X4),
-                        lhsT_scale=w_scales[:, chans],
-                        rhs=codes[:].bitcast(FP8X4),
-                        rhs_scale=scales[:],
-                        start=True,
-                        stop=True,
-                    )
-                    nc.vector.scalar_tensor_tensor(
-                        out=y[g][:, h, s, :],
-                        in0=mx_ps[:],
-                        scalar=1.0 / math.sqrt(HID),
-                        in1=bypass[h][:],
-                        op0=ALU.mult,
-                        op1=ALU.add,
-                    )
+                chans = slice(h * P, (h + 1) * P)
+                byp_ps = psum_byp.tile([P, GROUP], F32, name="byp_ps")
+                nc.tensor.matmul(
+                    out=byp_ps[:], lhsT=byp_w[kind][:, chans], rhs=sec["featT"][:], start=True, stop=True
+                )
+                byp_sb = work.tile([P, GROUP], F32, name="byp_sb")
+                nc.scalar.mul(out=byp_sb[:], in_=byp_ps[:], mul=1.0 / math.sqrt(INP))
+                mx_ps = psum_mx.tile([P, GROUP], F32, name="mx_ps")
+                nc.tensor.matmul_mx(
+                    out=mx_ps[:],
+                    lhsT=w_codes[:, chans].bitcast(FP8X4),
+                    lhsT_scale=w_scales[:, chans],
+                    rhs=sec["codes"][:].bitcast(FP8X4),
+                    rhs_scale=sec["scales"][:],
+                    start=True,
+                    stop=True,
+                )
+                nc.vector.scalar_tensor_tensor(
+                    out=y[g][:, h, s, :],
+                    in0=mx_ps[:],
+                    scalar=1.0 / math.sqrt(HID),
+                    in1=byp_sb[:],
+                    op0=ALU.mult,
+                    op1=ALU.add,
+                )
+
+            def statistics(sec):
+                g, s = sec["g"], sec["s"]
                 for h in range(HALVES):
                     if s == 0:
                         chunk = stats_scal[:, h, g, :]
@@ -205,18 +216,26 @@ def tile_feedforward_pb_t_kernel(
                         chunk = stats_vec[:, h, g * DV + s - 1, :]
                     nc.vector.bn_stats(out=chunk, in_=y[g][:, h, s, :])
 
-            todo = [(g, s) for g in range(GROUPS) for s in range(SECTIONS)]
-            load(0)
-            load(1)
-            ready = prepare(*todo[0])
-            for i in range(1, len(todo)):
-                g, s = todo[i]
-                if s == 0 and g + 1 < GROUPS:
-                    load(g + 1)
-                following = prepare(g, s)
-                multiply(todo[i - 1][0], todo[i - 1][1], ready)
-                ready = following
-            multiply(todo[-1][0], todo[-1][1], ready)
+            with tc.manual_schedule():
+                load(0)
+                load(1)
+                previous = None
+                for g in range(GROUPS):
+                    for s in range(SECTIONS):
+                        if s == 0 and 0 < g < GROUPS - 1:
+                            load(g + 1)
+                        current = open_section(g, s)
+                        for half in range(2):
+                            transpose_half(current, half)
+                            if previous is not None:
+                                multiply_half(previous, half)
+                        close_section(current)
+                        if previous is not None:
+                            statistics(previous)
+                        previous = current
+                for h in range(HALVES):
+                    multiply_half(previous, h)
+                statistics(previous)
 
         moments = consts.tile([P, 2 * HALVES, 2], F32)
         for h in range(HALVES):
@@ -300,9 +319,10 @@ def tile_feedforward_pb_t_kernel(
                 group_rows = out[g * GROUP : (g + 1) * GROUP, :].rearrange("(p j) c -> p j c", j=J)
                 nc.sync.dma_start(out=group_rows[:, 2 * half : 2 * half + 2, :], in_=rows_sb[:])
 
-            normalise(0)
-            for g in range(GROUPS):
-                if g + 1 < GROUPS:
-                    normalise(g + 1)
-                for half in range(2):
-                    store(g, half)
+            with tc.manual_schedule():
+                normalise(0)
+                for g in range(GROUPS):
+                    if g + 1 < GROUPS:
+                        normalise(g + 1)
+                    for half in range(2):
+                        store(g, half)

@@ -25,6 +25,7 @@ J = GROUP // P
 GROUPS = NODES // GROUP
 STATS = 6
 EPS = 1e-5
+LOOKAHEAD = 2
 
 FLOPS = 2 * NODES * SECTIONS * OUTC * (HID + INP)
 
@@ -87,7 +88,7 @@ def tile_feedforward_pb_t_kernel(
 
         with ExitStack() as phase1:
             stage = phase1.enter_context(tc.tile_pool(name="stage", bufs=2))
-            work = phase1.enter_context(tc.tile_pool(name="work", bufs=3))
+            work = phase1.enter_context(tc.tile_pool(name="work", bufs=LOOKAHEAD + 2))
             psum_x = phase1.enter_context(tc.psum_pool(name="psum_x", bufs=2))
             psum_f = phase1.enter_context(tc.psum_pool(name="psum_f", bufs=2))
             psum_mx = phase1.enter_context(tc.psum_pool(name="psum_mx", bufs=2))
@@ -125,7 +126,7 @@ def tile_feedforward_pb_t_kernel(
                     "g": g,
                     "s": s,
                     "hidden": hidden,
-                    "grouped": work.tile([P, GROUP, 2], F32, name="grouped", align_bytes=64),
+                    "grouped": work.tile([P, GROUP, 2], F32, name="grouped", bufs=2, align_bytes=64),
                     "feat_ps": psum_f.tile([P, GROUP], BF16, name="feat_ps"),
                 }
 
@@ -216,26 +217,29 @@ def tile_feedforward_pb_t_kernel(
                         chunk = stats_vec[:, h, g * DV + s - 1, :]
                     nc.vector.bn_stats(out=chunk, in_=y[g][:, h, s, :])
 
+            order = [(g, s) for g in range(GROUPS) for s in range(SECTIONS)]
+            sections = []
             with tc.manual_schedule():
                 load(0)
                 load(1)
-                previous = None
-                for g in range(GROUPS):
-                    for s in range(SECTIONS):
+                for i in range(len(order) + LOOKAHEAD):
+                    current = None
+                    if i < len(order):
+                        g, s = order[i]
                         if s == 0 and 0 < g < GROUPS - 1:
                             load(g + 1)
                         current = open_section(g, s)
-                        for half in range(2):
+                        sections.append(current)
+                    older = sections[i - LOOKAHEAD] if i >= LOOKAHEAD else None
+                    for half in range(2):
+                        if current is not None:
                             transpose_half(current, half)
-                            if previous is not None:
-                                multiply_half(previous, half)
+                        if older is not None:
+                            multiply_half(older, half)
+                    if current is not None:
                         close_section(current)
-                        if previous is not None:
-                            statistics(previous)
-                        previous = current
-                for h in range(HALVES):
-                    multiply_half(previous, h)
-                statistics(previous)
+                    if older is not None:
+                        statistics(older)
 
         moments = consts.tile([P, 2 * HALVES, 2], F32)
         for h in range(HALVES):
@@ -304,9 +308,9 @@ def tile_feedforward_pb_t_kernel(
                 nc.vector.tensor_copy(
                     out=rows_sb[:, :, 0:OUTC], in_=scal_ps[:].rearrange("p j h c -> p j (h c)")
                 )
-                for jj in range(2):
-                    nodes = slice((2 * half + jj) * P, (2 * half + jj + 1) * P)
-                    for h in range(HALVES):
+                for h in range(HALVES):
+                    for jj in range(2):
+                        nodes = slice((2 * half + jj) * P, (2 * half + jj + 1) * P)
                         vec_ps = psum_v.tile([P, DV, P], F32, name="vec_ps")
                         for d in range(DV):
                             nc.tensor.transpose(vec_ps[:, d, :], y[g][:, h, 1 + d, nodes], ident_f32[:])

from contextlib import ExitStack
import math

import concourse.mybir as mybir
from concourse.masks import make_identity

F32 = mybir.dt.float32
BF16 = mybir.dt.bfloat16
U32 = mybir.dt.uint32
U8 = mybir.dt.uint8
FP8X4 = mybir.dt.float8_e4m3fn_x4
ALU = mybir.AluOpType
ACT = mybir.ActivationFunctionType

P = 128
NODES = 4096
DV = 3
SECTIONS = 1 + DV
HID = 512
INP = 128
OUTC = 256
HALVES = OUTC // P
GROUP = 512
J = GROUP // P
GROUPS = NODES // GROUP
STATS = 6
EPS = 1e-5
LOOKAHEAD = 2

FLOPS = 2 * NODES * SECTIONS * OUTC * (HID + INP)


def quantise_weight(nc, pool, w, label):
    raw = pool.tile([P, 4, OUTC], BF16, name="w_raw")
    for u in range(2):
        nc.scalar.dma_start(
            out=raw[:, 2 * u : 2 * u + 2, :],
            in_=w[256 * u : 256 * (u + 1), :].rearrange("(p e) c -> p e c", e=2),
        )
    grouped = pool.tile([P, OUTC, 4], BF16, name="w_grouped", align_bytes=64)
    nc.vector.tensor_copy(out=grouped[:], in_=raw[:].rearrange("p t c -> p c t"))
    codes = pool.tile([P, OUTC], U32, name=label + "_codes", align_bytes=64)
    scales = pool.tile([P, OUTC], U8, name=label + "_scales", align_bytes=64)
    nc.vector.quantize_mx(
        out=codes[:].bitcast(FP8X4),
        scales=scales[:],
        in_=grouped[:].rearrange("p c t -> p (c t)"),
    )
    return codes, scales


def tile_feedforward_pb_t_kernel(
    tc, h2, features, lin3_W0, lin3_W1, byp_W0, byp_W1, bn_weight, bn_bias, out
):
    nc = tc.nc
    with ExitStack() as whole:
        consts = whole.enter_context(tc.tile_pool(name="consts", bufs=1))
        y_pool = whole.enter_context(tc.tile_pool(name="y", bufs=1))

        ident_f32 = consts.tile([P, P], F32)
        make_identity(nc, ident_f32[:])
        ident_bf16 = consts.tile([P, P], BF16)
        make_identity(nc, ident_bf16[:])

        warm = consts.tile([P, 1], F32)
        nc.vector.memset(warm[:], 1.0)
        nc.scalar.sqrt(out=warm[:], in_=warm[:])

        lin_w = [
            quantise_weight(nc, consts, lin3_W0, "w0"),
            quantise_weight(nc, consts, lin3_W1, "w1"),
        ]
        byp_w = []
        for label, w in (("byp0", byp_W0), ("byp1", byp_W1)):
            w_sb = consts.tile([P, OUTC], BF16, name=label)
            nc.scalar.dma_start(out=w_sb[:], in_=w)
            byp_w.append(w_sb)

        bn_rows = consts.tile([P, P], BF16)
        nc.vector.memset(bn_rows[:], 0.0)
        nc.scalar.dma_start(out=bn_rows[0:4, :], in_=bn_weight.rearrange("(r c) -> r c", c=P))
        nc.scalar.dma_start(out=bn_rows[4:6, :], in_=bn_bias.rearrange("(r c) -> r c", c=P))
        bn_cols = consts.tile([P, 6], F32)

        y = [y_pool.tile([P, HALVES, SECTIONS, GROUP], F32, name="y%d" % g) for g in range(GROUPS)]
        stats_scal = consts.tile([P, HALVES, GROUPS, STATS], F32)
        stats_vec = consts.tile([P, HALVES, GROUPS * DV, STATS], F32)

        with ExitStack() as phase1:
            stage = phase1.enter_context(tc.tile_pool(name="stage", bufs=2))
            work = phase1.enter_context(tc.tile_pool(name="work", bufs=LOOKAHEAD + 2))
            psum_x = phase1.enter_context(tc.psum_pool(name="psum_x", bufs=2))
            psum_f = phase1.enter_context(tc.psum_pool(name="psum_f", bufs=2))
            psum_mx = phase1.enter_context(tc.psum_pool(name="psum_mx", bufs=2))
            psum_byp = phase1.enter_context(tc.psum_pool(name="psum_byp", bufs=2))

            bn_ps = psum_f.tile([P, P], BF16, tag="feat_ps")
            nc.tensor.transpose(bn_ps[:], bn_rows[:], ident_bf16[:])
            nc.vector.tensor_copy(out=bn_cols[:], in_=bn_ps[:, 0:6])

            loaded = {}

            def load(g):
                rows = slice(g * GROUP, (g + 1) * GROUP)
                h2_scal = stage.tile([P, J, HID], BF16, name="h2_scal")
                nc.sync.dma_start(
                    out=h2_scal[:], in_=h2[rows, 0:HID].rearrange("(p j) k -> p j k", j=J)
                )
                feat = stage.tile([P, J, SECTIONS * INP], BF16, name="feat")
                nc.sync.dma_start(
                    out=feat[:], in_=features[rows, :].rearrange("(p j) k -> p j k", j=J)
                )
                h2_vec = stage.tile([P, J, DV * HID], BF16, name="h2_vec")
                nc.sync.dma_start(
                    out=h2_vec[:], in_=h2[rows, HID:].rearrange("(p j) k -> p j k", j=J)
                )
                loaded[g] = (h2_scal, feat, h2_vec)

            def open_section(g, s):
                h2_scal, feat, h2_vec = loaded[g]
                if s == 0:
                    hidden = h2_scal
                else:
                    hidden = stage.tile([P, J, HID], BF16, name="h2_comp", bufs=5)
                return {
                    "g": g,
                    "s": s,
                    "hidden": hidden,
                    "grouped": work.tile([P, GROUP, 2], F32, name="grouped", bufs=2, align_bytes=64),
                    "feat_ps": psum_f.tile([P, GROUP], BF16, name="feat_ps"),
                }

            def transpose_half(sec, half):
                h2_scal, feat, h2_vec = loaded[sec["g"]]
                s = sec["s"]
                hidden = sec["hidden"]
                pair = slice(2 * half, 2 * half + 2)
                if s > 0:
                    nc.gpsimd.tensor_scalar(
                        out=hidden[:, pair, :],
                        in0=h2_vec[:, pair, :].rearrange("p j (i d) -> p d j i", d=DV)[:, s - 1],
                        scalar1=1.0,
                        scalar2=0.0,
                        op0=ALU.mult,
                        op1=ALU.add,
                    )
                hid_ps = psum_x.tile([P, 2, 2 * P], F32, name="hid_ps")
                for jj in range(2):
                    words = hidden[:, 2 * half + jj, :].bitcast(F32)
                    for u in range(2):
                        nc.tensor.transpose(
                            hid_ps[:, u, jj * P : (jj + 1) * P],
                            words[:, u * P : (u + 1) * P],
                            ident_f32[:],
                        )
                nc.scalar.copy(
                    out=sec["grouped"][:, half * 2 * P : (half + 1) * 2 * P, :],
                    in_=hid_ps[:].rearrange("p u n -> p n u"),
                )
                for j in range(2 * half, 2 * half + 2):
                    if s == 0:
                        cols = feat[:, j, 0:INP]
                    else:
                        cols = feat[:, j, INP:].rearrange("p (i d) -> p d i", d=DV)[:, s - 1]
                    nc.tensor.transpose(sec["feat_ps"][:, j * P : (j + 1) * P], cols, ident_bf16[:])

            def close_section(sec):
                featT = work.tile([P, GROUP], BF16, name="featT")
                nc.scalar.copy(out=featT[:], in_=sec["feat_ps"][:])
                codes = work.tile([P, GROUP], U32, name="codes", align_bytes=64)
                scales = work.tile([P, GROUP], U8, name="scales", align_bytes=64)
                nc.vector.quantize_mx(
                    out=codes[:].bitcast(FP8X4),
                    scales=scales[:],
                    in_=sec["grouped"][:].rearrange("p n w -> p (n w)").bitcast(BF16),
                )
                sec["featT"] = featT
                sec["codes"] = codes
                sec["scales"] = scales

            def multiply_half(sec, h):
                g, s = sec["g"], sec["s"]
                kind = min(s, 1)
                w_codes, w_scales = lin_w[kind]
                chans = slice(h * P, (h + 1) * P)
                byp_ps = psum_byp.tile([P, GROUP], F32, name="byp_ps")
                nc.tensor.matmul(
                    out=byp_ps[:], lhsT=byp_w[kind][:, chans], rhs=sec["featT"][:], start=True, stop=True
                )
                byp_sb = work.tile([P, GROUP], F32, name="byp_sb")
                nc.scalar.mul(out=byp_sb[:], in_=byp_ps[:], mul=1.0 / math.sqrt(INP))
                mx_ps = psum_mx.tile([P, GROUP], F32, name="mx_ps")
                nc.tensor.matmul_mx(
                    out=mx_ps[:],
                    lhsT=w_codes[:, chans].bitcast(FP8X4),
                    lhsT_scale=w_scales[:, chans],
                    rhs=sec["codes"][:].bitcast(FP8X4),
                    rhs_scale=sec["scales"][:],
                    start=True,
                    stop=True,
                )
                nc.vector.scalar_tensor_tensor(
                    out=y[g][:, h, s, :],
                    in0=mx_ps[:],
                    scalar=1.0 / math.sqrt(HID),
                    in1=byp_sb[:],
                    op0=ALU.mult,
                    op1=ALU.add,
                )

            def statistics(sec):
                g, s = sec["g"], sec["s"]
                for h in range(HALVES):
                    if s == 0:
                        chunk = stats_scal[:, h, g, :]
                    else:
                        chunk = stats_vec[:, h, g * DV + s - 1, :]
                    nc.vector.bn_stats(out=chunk, in_=y[g][:, h, s, :])

            order = [(g, s) for g in range(GROUPS) for s in range(SECTIONS)]
            sections = []
            with tc.manual_schedule():
                load(0)
                load(1)
                for i in range(len(order) + LOOKAHEAD):
                    current = None
                    if i < len(order):
                        g, s = order[i]
                        if s == 0 and 0 < g < GROUPS - 1:
                            load(g + 1)
                        current = open_section(g, s)
                        sections.append(current)
                    older = sections[i - LOOKAHEAD] if i >= LOOKAHEAD else None
                    for half in range(2):
                        if current is not None:
                            transpose_half(current, half)
                        if older is not None:
                            multiply_half(older, half)
                    if current is not None:
                        close_section(current)
                    if older is not None:
                        statistics(older)

        moments = consts.tile([P, 2 * HALVES, 2], F32)
        for h in range(HALVES):
            nc.vector.bn_aggr(
                out=moments[:, h, :], in_=stats_scal[:, h].rearrange("p c s -> p (c s)")
            )
            nc.vector.bn_aggr(
                out=moments[:, HALVES + h, :], in_=stats_vec[:, h].rearrange("p c s -> p (c s)")
            )
        mean_sq = consts.tile([P, HALVES], F32)
        nc.vector.tensor_mul(out=mean_sq[:], in0=moments[:, HALVES:, 0], in1=moments[:, HALVES:, 0])
        spread = consts.tile([P, 2 * HALVES], F32)
        nc.vector.tensor_scalar_add(out=spread[:, 0:HALVES], in0=moments[:, 0:HALVES, 1], scalar1=EPS)
        nc.vector.scalar_tensor_tensor(
            out=spread[:, HALVES:],
            in0=moments[:, HALVES:, 1],
            scalar=EPS,
            in1=mean_sq[:],
            op0=ALU.add,
            op1=ALU.add,
        )
        root = consts.tile([P, 2 * HALVES], F32)
        nc.scalar.sqrt(out=root[:], in_=spread[:])
        scale = consts.tile([P, 2 * HALVES], F32)
        nc.vector.reciprocal(out=scale[:], in_=root[:])
        nc.vector.tensor_mul(out=scale[:], in0=scale[:], in1=bn_cols[:, 0 : 2 * HALVES])
        shift = consts.tile([P, 2 * HALVES], F32)
        nc.vector.memset(shift[:], 0.0)
        scaled_mean = consts.tile([P, HALVES], F32)
        nc.vector.tensor_mul(out=scaled_mean[:], in0=moments[:, 0:HALVES, 0], in1=scale[:, 0:HALVES])
        nc.vector.tensor_sub(
            out=shift[:, 0:HALVES], in0=bn_cols[:, 2 * HALVES : 3 * HALVES], in1=scaled_mean[:]
        )

        with ExitStack() as phase2:
            rows_pool = phase2.enter_context(tc.tile_pool(name="rows", bufs=3))
            psum_s = phase2.enter_context(tc.psum_pool(name="psum_s", bufs=2))
            psum_v = phase2.enter_context(tc.psum_pool(name="psum_v", bufs=6))

            def normalise(g):
                for h in range(HALVES):
                    nc.scalar.activation(
                        out=y[g][:, h, 0, :],
                        in_=y[g][:, h, 0, :],
                        func=ACT.Identity,
                        scale=scale[:, h : h + 1],
                        bias=shift[:, h : h + 1],
                    )
                    b = HALVES + h
                    nc.gpsimd.tensor_scalar(
                        out=y[g][:, h, 1:, :],
                        in0=y[g][:, h, 1:, :],
                        scalar1=scale[:, b : b + 1],
                        scalar2=shift[:, b : b + 1],
                        op0=ALU.mult,
                        op1=ALU.add,
                    )

            def store(g, half):
                rows_sb = rows_pool.tile([P, 2, SECTIONS * OUTC], F32, name="rows_sb")
                scal_ps = psum_s.tile([P, 2, HALVES, P], F32, name="scal_ps")
                for jj in range(2):
                    nodes = slice((2 * half + jj) * P, (2 * half + jj + 1) * P)
                    for h in range(HALVES):
                        nc.tensor.transpose(scal_ps[:, jj, h, :], y[g][:, h, 0, nodes], ident_f32[:])
                nc.vector.tensor_copy(
                    out=rows_sb[:, :, 0:OUTC], in_=scal_ps[:].rearrange("p j h c -> p j (h c)")
                )
                for h in range(HALVES):
                    for jj in range(2):
                        nodes = slice((2 * half + jj) * P, (2 * half + jj + 1) * P)
                        vec_ps = psum_v.tile([P, DV, P], F32, name="vec_ps")
                        for d in range(DV):
                            nc.tensor.transpose(vec_ps[:, d, :], y[g][:, h, 1 + d, nodes], ident_f32[:])
                        first = OUTC + h * DV * P
                        dest = rows_sb[:, jj, first : first + DV * P].rearrange("p (o d) -> p o d", d=DV)
                        if h == 0:
                            nc.vector.tensor_copy(out=dest, in_=vec_ps[:].rearrange("p d o -> p o d"))
                        else:
                            nc.scalar.copy(out=dest, in_=vec_ps[:].rearrange("p d o -> p o d"))
                group_rows = out[g * GROUP : (g + 1) * GROUP, :].rearrange("(p j) c -> p j c", j=J)
                nc.sync.dma_start(out=group_rows[:, 2 * half : 2 * half + 2, :], in_=rows_sb[:])

            with tc.manual_schedule():
                normalise(0)
                for g in range(GROUPS):
                    if g + 1 < GROUPS:
                        normalise(g + 1)
                    for half in range(2):
                        store(g, half)
